import numpy as np
import ml_dtypes


def mxq(x, axis, fmt="e4m3"):
    dtype, down = {"e4m3": (ml_dtypes.float8_e4m3fn, 7), "e5m2": (ml_dtypes.float8_e5m2, 14)}[fmt]
    v = np.moveaxis(np.asarray(x, np.float32).astype(ml_dtypes.bfloat16).astype(np.float64), axis, -1)
    blocks = v.reshape(v.shape[:-1] + (-1, 32))
    amax = np.abs(blocks).max(-1, keepdims=True)
    byte = np.maximum(np.where(amax > 0, np.frexp(amax)[1] - 1 + 127, 0) - down, 1)
    scale = np.exp2(byte - 127.0)
    codes = (blocks / scale).astype(np.float32).astype(dtype).astype(np.float64)
    return np.moveaxis((codes * scale).reshape(v.shape), -1, axis)


WIDE = False


def mx_kscale(k):
    if not WIDE:
        return np.ones(k)
    levels = np.array([10, -10, 5, -5, 0])
    a = np.random.permutation(np.resize(levels, k // 512 * 4)).reshape(k // 512, 4)
    idx = np.arange(k)
    return np.exp2(a[idx // 512, idx % 128 // 32])


BF16 = ml_dtypes.bfloat16


def bf(x):
    return np.asarray(x, np.float32).astype(BF16)


def f64(x):
    return np.asarray(x).astype(np.float64)


B, S, K, N = 4, 128, 2048, 4096
THRESHOLD = 0.3


def ternary_quantize(w, threshold=THRESHOLD):
    return np.sign(w) * (np.abs(w) > threshold)


def ternary_ste(w, threshold=THRESHOLD):
    return w + (ternary_quantize(w, threshold) - w)


def setup_inputs():
    s = mx_kscale(K)
    r = s / s.min()
    return {"x": bf(np.random.standard_normal((B, S, K)) * 8.0 / np.sqrt(K) * r),
            "kernel": bf(0.2 * np.random.standard_normal((K, N)) / r[:, None])}


def reference(x, kernel):
    w_ternary = ternary_ste(f64(kernel), THRESHOLD)
    return mxq(f64(x), 2, "e4m3") @ mxq(w_ternary, 0, "e4m3")

@@ -1,0 +1,210 @@
+from contextlib import ExitStack
+
+import concourse.mybir as mybir
+from concourse.masks import make_identity
+
+FLOPS = 2 * 512 * 2048 * 4096
+
+BF16 = mybir.dt.bfloat16
+F32 = mybir.dt.float32
+I32 = mybir.dt.int32
+U32 = mybir.dt.uint32
+U8 = mybir.dt.uint8
+FP8X4 = mybir.dt.float8_e4m3fn_x4
+ALU = mybir.AluOpType
+ACT = mybir.ActivationFunctionType
+
+P = 128
+NCH = 8
+CW = 512
+G = 4
+MT = 4
+INV = 1.0 / 0.6
+CS = 192
+MANUAL = True
+
+
+def tile_ternarylinear_kernel(tc, x, kernel, out):
+    nc = tc.nc
+    with ExitStack() as ctx:
+        const = ctx.enter_context(tc.tile_pool(name="const", bufs=1))
+        xraw = ctx.enter_context(tc.tile_pool(name="xraw", bufs=1))
+        xgp = ctx.enter_context(tc.tile_pool(name="xgp", bufs=2))
+        rawu = ctx.enter_context(tc.tile_pool(name="rawu", bufs=8))
+        raws = ctx.enter_context(tc.tile_pool(name="raws", bufs=8))
+        tmpv = ctx.enter_context(tc.tile_pool(name="tmpv", bufs=2))
+        tmps = ctx.enter_context(tc.tile_pool(name="tmps", bufs=1))
+        grpv = ctx.enter_context(tc.tile_pool(name="grpv", bufs=3))
+        grpm = ctx.enter_context(tc.tile_pool(name="grpm", bufs=2))
+        grps = ctx.enter_context(tc.tile_pool(name="grps", bufs=2))
+        codp = ctx.enter_context(tc.tile_pool(name="codp", bufs=6))
+        stgp = ctx.enter_context(tc.tile_pool(name="stgp", bufs=3))
+        psum = ctx.enter_context(tc.psum_pool(name="psum", bufs=1))
+        if MANUAL:
+            ctx.enter_context(tc.manual_schedule())
+
+        ident = const.tile([P, P], F32, name="ident")
+        make_identity(nc, ident[:])
+        xq = const.tile([P, MT, 512], U32, name="xq", align_bytes=64)
+        xs = const.tile([P, MT, 512], U8, name="xs", align_bytes=64)
+
+        xr = []
+        for mt in range(MT):
+            t = xraw.tile([P, 2048], BF16, name="xr%d" % mt)
+            nc.sync.dma_start(out=t[:], in_=x[mt])
+            xr.append(t)
+
+        raw = {}
+
+        def load_w(g, c0, ncols, pool, tag):
+            t = pool.tile([P, 4, ncols], BF16, name=tag, tag=tag)
+            nc.sync.dma_start(
+                out=t[:],
+                in_=kernel[512 * g : 512 * (g + 1), c0 : c0 + ncols].rearrange("(p t) c -> p t c", t=4),
+            )
+            for k in range(ncols // CW):
+                raw[(c0 // CW + k, g)] = (t, k * CW)
+
+        for j in range(2):
+            for g in (0, 3, 1, 2):
+                load_w(g, j * CW, CW, rawu, "rawu")
+        for jj in (1, 2):
+            for g in (0, 3, 1, 2):
+                load_w(g, jj * 2 * CW, 2 * CW, raws, "raws")
+
+        xg = []
+
+        def quant_x(mt):
+            nc.vector.quantize_mx(out=xq[:, mt, :].bitcast(FP8X4), scales=xs[:, mt, :], in_=xg[mt][:])
+
+        for mt in range(MT):
+            xw = xr[mt][:].bitcast(F32).rearrange("p (g w u) -> p g u w", g=G, u=2)
+            xgt = xgp.tile([P, 2048], BF16, name="xg", tag="xg", align_bytes=64)
+            xg.append(xgt)
+            for h in range(2):
+                bank = psum.tile([P, 4, P], F32, name="xb%d" % (2 * mt + h), tag="bank%d" % (2 * mt + h))
+                for a in range(2):
+                    for u in range(2):
+                        nc.tensor.transpose(bank[:, 2 * a + u, :], xw[:, 2 * h + a, u, :], ident[:])
+                dst = xgt[:].bitcast(F32)[:, 512 * h : 512 * (h + 1)].rearrange("p (a m u) -> p a m u", a=2, u=2)
+                src = bank[:].rearrange("p (a u) m -> p a m u", a=2, u=2)
+                if h == 0:
+                    nc.scalar.copy(out=dst, in_=src)
+                else:
+                    nc.vector.tensor_copy(out=dst, in_=src)
+            if mt >= 1:
+                quant_x(mt - 1)
+        quant_x(MT - 1)
+
+        grp = {}
+        tmp_of = {}
+        acc = {}
+        vunits = []
+        for j in range(NCH):
+            vunits += [(j, 0, CW), (j, 1, CW), (j, 2, CW - CS)]
+        NV = len(vunits)
+
+        def scalar_first(j, g, c0, ncols, tag):
+            rt, o = raw[(j, g)]
+            t = tmps.tile([P, 4, ncols], U32, name=tag, tag=tag)
+            nc.scalar.activation(out=t[:], in_=rt[:, :, o + c0 : o + c0 + ncols], func=ACT.Relu, bias=1.0, scale=INV)
+            return t
+
+        def scalar_second(t, gt, c0, ncols):
+            nc.scalar.activation(
+                out=gt[:, c0 : c0 + ncols, :], in_=t[:].rearrange("p t c -> p c t"), func=ACT.Sign, bias=-1.0, scale=1.0
+            )
+
+        def scalar_units(j):
+            t3 = scalar_first(j, 3, 0, CW, "ts3")
+            t2 = scalar_first(j, 2, CW - CS, CS, "ts2")
+            g3 = grps.tile([P, CW, 4], BF16, name="g3", tag="g3", align_bytes=64)
+            g2 = grpm.tile([P, CW, 4], BF16, name="g2", tag="g2", align_bytes=64)
+            grp[(j, 3)] = g3
+            grp[(j, 2)] = g2
+            scalar_second(t3, g3, 0, CW)
+            scalar_second(t2, g2, CW - CS, CS)
+
+        def vec_first(n):
+            j, g, ncols = vunits[n]
+            rt, o = raw[(j, g)]
+            t = tmpv.tile([P, 4, CW], I32, name="tv", tag="tv")
+            nc.vector.tensor_scalar(
+                out=t[:, :, 0:ncols], in0=rt[:, :, o : o + ncols], scalar1=INV, scalar2=-1.0, op0=ALU.mult, op1=ALU.max
+            )
+            tmp_of[n] = t
+
+        def vec_second(n):
+            j, g, ncols = vunits[n]
+            if g != 2:
+                grp[(j, g)] = grpv.tile([P, CW, 4], BF16, name="gv", tag="gv", align_bytes=64)
+            nc.vector.tensor_scalar(
+                out=grp[(j, g)][:, 0:ncols, :],
+                in0=tmp_of[n][:, :, 0:ncols].rearrange("p t c -> p c t"),
+                scalar1=1.0,
+                scalar2=None,
+                op0=ALU.min,
+            )
+
+        def quant_and_multiply(j, g, order):
+            cod = codp.tile([P, CW], U32, name="cod", tag="cod", align_bytes=64)
+            scl = codp.tile([P, CW], U8, name="scl", tag="scl", align_bytes=64)
+            nc.vector.quantize_mx(out=cod[:].bitcast(FP8X4), scales=scl[:], in_=grp[(j, g)][:].rearrange("p c t -> p (c t)"))
+            if g == 0:
+                acc[j] = [
+                    psum.tile([P, CW], F32, name="acc%d" % (4 * (j % 2) + mt), tag="bank%d" % (4 * (j % 2) + mt))
+                    for mt in range(MT)
+                ]
+            for mt in order:
+                nc.tensor.matmul_mx(
+                    out=acc[j][mt][:],
+                    lhsT=xq[:, mt, P * g : P * (g + 1)].bitcast(FP8X4),
+                    lhsT_scale=xs[:, mt, P * g : P * (g + 1)],
+                    rhs=cod[:].bitcast(FP8X4),
+                    rhs_scale=scl[:],
+                    start=(g == 0),
+                    stop=(g == 2),
+                )
+
+        def step(n):
+            if n < NV:
+                vec_first(n)
+            if 0 <= n - 1 < NV:
+                vec_second(n - 1)
+            if 0 <= n - 2 < NV:
+                j, g, ncols = vunits[n - 2]
+                order = (0, 2, 1, 3) if (j == NCH - 1 and g == 2) else (0, 1, 2, 3)
+                quant_and_multiply(j, g, order)
+                if g == 1:
+                    quant_and_multiply(j, 3, (0, 1, 2, 3))
+
+        def out_cols(j):
+            return out[:, :, CW * j : CW * (j + 1)].rearrange("b s n -> s b n")
+
+        def evacuate(j):
+            st = stgp.tile([P, MT, CW], F32, name="st", tag="st")
+            for mt in range(MT):
+                nc.scalar.copy(out=st[:, mt, :], in_=acc[j][mt][:])
+            nc.sync.dma_start(out=out_cols(j), in_=st[:])
+
+        for j in range(NCH):
+            scalar_units(j)
+            for n in (3 * j, 3 * j + 1, 3 * j + 2):
+                step(n)
+            if j == 3:
+                for g in (0, 3, 1, 2):
+                    load_w(g, 3 * 2 * CW, 2 * CW, raws, "raws")
+            if j >= 1:
+                evacuate(j - 1)
+        step(NV)
+        step(NV + 1)
+
+        j = NCH - 1
+        sa = stgp.tile([P, 2, CW], F32, name="sa", tag="st")
+        sb = stgp.tile([P, 2, CW], F32, name="sb", tag="st")
+        nc.scalar.copy(out=sa[:, 0, :], in_=acc[j][0][:])
+        nc.vector.tensor_copy(out=sb[:, 0, :], in_=acc[j][2][:])
+        nc.scalar.copy(out=sa[:, 1, :], in_=acc[j][1][:])
+        nc.vector.tensor_copy(out=sb[:, 1, :], in_=acc[j][3][:])
+        nc.sync.dma_start(out=out_cols(j)[:, 0:2, :], in_=sa[:])
+        nc.sync.dma_start(out=out_cols(j)[:, 2:4, :], in_=sb[:])

@@ -112,7 +112,11 @@ def tile_ternarylinear_kernel(tc, x, kernel, out):
 
         def scalar_second(t, gt, c0, ncols):
             nc.scalar.activation(
-                out=gt[:, c0 : c0 + ncols, :], in_=t[:].rearrange("p t c -> p c t"), func=ACT.Sign, bias=-1.0, scale=1.0
+                out=gt[:, c0 : c0 + ncols, :].rearrange("p (c i) t -> p c t i", i=4),
+                in_=t[:].rearrange("p t (c i) -> p c t i", i=4),
+                func=ACT.Sign,
+                bias=-1.0,
+                scale=1.0,
             )
 
         def scalar_units(j):
@@ -139,8 +143,8 @@ def tile_ternarylinear_kernel(tc, x, kernel, out):
             if g != 2:
                 grp[(j, g)] = grpv.tile([P, CW, 4], BF16, name="gv", tag="gv", align_bytes=64)
             nc.vector.tensor_scalar(
-                out=grp[(j, g)][:, 0:ncols, :],
-                in0=tmp_of[n][:, :, 0:ncols].rearrange("p t c -> p c t"),
+                out=grp[(j, g)][:, 0:ncols, :].rearrange("p (c i) t -> p c t i", i=4),
+                in0=tmp_of[n][:, :, 0:ncols].rearrange("p t (c i) -> p c t i", i=4),
                 scalar1=1.0,
                 scalar2=None,
                 op0=ALU.min,

@@ -15,21 +15,26 @@ ALU = mybir.AluOpType
 ACT = mybir.ActivationFunctionType
 
 P = 128
-NCH = 8
 CW = 512
 G = 4
 MT = 4
 INV = 1.0 / 0.6
-CS = 192
-MANUAL = True
+WIDTHS = (512, 512, 512, 512, 512, 512, 512, 256, 256)
+NCH = 9
+COL0 = (0, 512, 1024, 1536, 2048, 2560, 3072, 3584, 3840)
+CS = 176
+LOAD_ORDER = (0, 3, 1, 2)
+
+
+def scalar_share(j):
+    return CS * WIDTHS[j] // CW
 
 
 def tile_ternarylinear_kernel(tc, x, kernel, out):
     nc = tc.nc
     with ExitStack() as ctx:
         const = ctx.enter_context(tc.tile_pool(name="const", bufs=1))
-        xraw = ctx.enter_context(tc.tile_pool(name="xraw", bufs=1))
-        xgp = ctx.enter_context(tc.tile_pool(name="xgp", bufs=2))
+        xgp = ctx.enter_context(tc.tile_pool(name="xgp", bufs=4))
         rawu = ctx.enter_context(tc.tile_pool(name="rawu", bufs=8))
         raws = ctx.enter_context(tc.tile_pool(name="raws", bufs=8))
         tmpv = ctx.enter_context(tc.tile_pool(name="tmpv", bufs=2))
@@ -37,47 +42,40 @@ def tile_ternarylinear_kernel(tc, x, kernel, out):
         grpv = ctx.enter_context(tc.tile_pool(name="grpv", bufs=3))
         grpm = ctx.enter_context(tc.tile_pool(name="grpm", bufs=2))
         grps = ctx.enter_context(tc.tile_pool(name="grps", bufs=2))
-        codp = ctx.enter_context(tc.tile_pool(name="codp", bufs=6))
-        stgp = ctx.enter_context(tc.tile_pool(name="stgp", bufs=3))
+        codp = ctx.enter_context(tc.tile_pool(name="codp", bufs=8))
+        stgp = ctx.enter_context(tc.tile_pool(name="stgp", bufs=6))
         psum = ctx.enter_context(tc.psum_pool(name="psum", bufs=1))
-        if MANUAL:
-            ctx.enter_context(tc.manual_schedule())
+        ctx.enter_context(tc.manual_schedule())
 
         ident = const.tile([P, P], F32, name="ident")
         make_identity(nc, ident[:])
         xq = const.tile([P, MT, 512], U32, name="xq", align_bytes=64)
         xs = const.tile([P, MT, 512], U8, name="xs", align_bytes=64)
 
-        xr = []
-        for mt in range(MT):
-            t = xraw.tile([P, 2048], BF16, name="xr%d" % mt)
-            nc.sync.dma_start(out=t[:], in_=x[mt])
-            xr.append(t)
-
         raw = {}
 
-        def load_w(g, c0, ncols, pool, tag):
+        def load_w(g, chunks, pool, tag):
+            c0 = COL0[chunks[0]]
+            ncols = sum(WIDTHS[j] for j in chunks)
             t = pool.tile([P, 4, ncols], BF16, name=tag, tag=tag)
             nc.sync.dma_start(
                 out=t[:],
                 in_=kernel[512 * g : 512 * (g + 1), c0 : c0 + ncols].rearrange("(p t) c -> p t c", t=4),
             )
-            for k in range(ncols // CW):
-                raw[(c0 // CW + k, g)] = (t, k * CW)
+            for j in chunks:
+                raw[(j, g)] = (t, COL0[j] - c0)
 
-        for j in range(2):
-            for g in (0, 3, 1, 2):
-                load_w(g, j * CW, CW, rawu, "rawu")
-        for jj in (1, 2):
-            for g in (0, 3, 1, 2):
-                load_w(g, jj * 2 * CW, 2 * CW, raws, "raws")
+        for g in LOAD_ORDER:
+            load_w(g, (0,), rawu, "rawu")
+        xr = []
+        for mt in range(MT):
+            t = rawu.tile([P, 2048], BF16, name="rawu", tag="rawu")
+            nc.sync.dma_start(out=t[:], in_=x[mt])
+            xr.append(t)
 
         xg = []
 
-        def quant_x(mt):
-            nc.vector.quantize_mx(out=xq[:, mt, :].bitcast(FP8X4), scales=xs[:, mt, :], in_=xg[mt][:])
-
-        for mt in range(MT):
+        def transpose_x(mt):
             xw = xr[mt][:].bitcast(F32).rearrange("p (g w u) -> p g u w", g=G, u=2)
             xgt = xgp.tile([P, 2048], BF16, name="xg", tag="xg", align_bytes=64)
             xg.append(xgt)
@@ -87,21 +85,19 @@ def tile_ternarylinear_kernel(tc, x, kernel, out):
                     for u in range(2):
                         nc.tensor.transpose(bank[:, 2 * a + u, :], xw[:, 2 * h + a, u, :], ident[:])
                 dst = xgt[:].bitcast(F32)[:, 512 * h : 512 * (h + 1)].rearrange("p (a m u) -> p a m u", a=2, u=2)
-                src = bank[:].rearrange("p (a u) m -> p a m u", a=2, u=2)
-                if h == 0:
-                    nc.scalar.copy(out=dst, in_=src)
-                else:
-                    nc.vector.tensor_copy(out=dst, in_=src)
-            if mt >= 1:
-                quant_x(mt - 1)
-        quant_x(MT - 1)
+                nc.scalar.copy(out=dst, in_=bank[:].rearrange("p (a u) m -> p a m u", a=2, u=2))
+
+        def quant_x(mt):
+            nc.vector.quantize_mx(out=xq[:, mt, :].bitcast(FP8X4), scales=xs[:, mt, :], in_=xg[mt][:])
 
         grp = {}
         tmp_of = {}
         acc = {}
+        held = []
+        x_ready = [False]
         vunits = []
         for j in range(NCH):
-            vunits += [(j, 0, CW), (j, 1, CW), (j, 2, CW - CS)]
+            vunits += [(j, 0, WIDTHS[j]), (j, 1, WIDTHS[j]), (j, 2, WIDTHS[j] - scalar_share(j))]
         NV = len(vunits)
 
         def scalar_first(j, g, c0, ncols, tag):
@@ -120,14 +116,16 @@ def tile_ternarylinear_kernel(tc, x, kernel, out):
             )
 
         def scalar_units(j):
-            t3 = scalar_first(j, 3, 0, CW, "ts3")
-            t2 = scalar_first(j, 2, CW - CS, CS, "ts2")
+            w = WIDTHS[j]
+            cs = scalar_share(j)
+            t3 = scalar_first(j, 3, 0, w, "ts3")
+            t2 = scalar_first(j, 2, w - cs, cs, "ts2")
             g3 = grps.tile([P, CW, 4], BF16, name="g3", tag="g3", align_bytes=64)
             g2 = grpm.tile([P, CW, 4], BF16, name="g2", tag="g2", align_bytes=64)
             grp[(j, 3)] = g3
             grp[(j, 2)] = g2
-            scalar_second(t3, g3, 0, CW)
-            scalar_second(t2, g2, CW - CS, CS)
+            scalar_second(t3, g3, 0, w)
+            scalar_second(t2, g2, w - cs, cs)
 
         def vec_first(n):
             j, g, ncols = vunits[n]
@@ -150,25 +148,36 @@ def tile_ternarylinear_kernel(tc, x, kernel, out):
                 op0=ALU.min,
             )
 
-        def quant_and_multiply(j, g, order):
-            cod = codp.tile([P, CW], U32, name="cod", tag="cod", align_bytes=64)
-            scl = codp.tile([P, CW], U8, name="scl", tag="scl", align_bytes=64)
-            nc.vector.quantize_mx(out=cod[:].bitcast(FP8X4), scales=scl[:], in_=grp[(j, g)][:].rearrange("p c t -> p (c t)"))
+        def multiply(j, g, cod, scl):
+            w = WIDTHS[j]
             if g == 0:
                 acc[j] = [
                     psum.tile([P, CW], F32, name="acc%d" % (4 * (j % 2) + mt), tag="bank%d" % (4 * (j % 2) + mt))
                     for mt in range(MT)
                 ]
+            order = (0, 2, 1, 3) if (j == NCH - 1 and g == 2) else (0, 1, 2, 3)
             for mt in order:
                 nc.tensor.matmul_mx(
-                    out=acc[j][mt][:],
+                    out=acc[j][mt][:, 0:w],
                     lhsT=xq[:, mt, P * g : P * (g + 1)].bitcast(FP8X4),
                     lhsT_scale=xs[:, mt, P * g : P * (g + 1)],
-                    rhs=cod[:].bitcast(FP8X4),
-                    rhs_scale=scl[:],
+                    rhs=cod[:, 0:w].bitcast(FP8X4),
+                    rhs_scale=scl[:, 0:w],
                     start=(g == 0),
                     stop=(g == 2),
                 )
+
+        def quant(j, g):
+            w = WIDTHS[j]
+            cod = codp.tile([P, CW], U32, name="cod", tag="cod", align_bytes=64)
+            scl = codp.tile([P, CW], U8, name="scl", tag="scl", align_bytes=64)
+            nc.vector.quantize_mx(
+                out=cod[:, 0:w].bitcast(FP8X4), scales=scl[:, 0:w], in_=grp[(j, g)][:, 0:w, :].rearrange("p c t -> p (c t)")
+            )
+            if x_ready[0]:
+                multiply(j, g, cod, scl)
+            else:
+                held.append((j, g, cod, scl))
 
         def step(n):
             if n < NV:
@@ -177,38 +186,67 @@ def tile_ternarylinear_kernel(tc, x, kernel, out):
                 vec_second(n - 1)
             if 0 <= n - 2 < NV:
                 j, g, ncols = vunits[n - 2]
-                order = (0, 2, 1, 3) if (j == NCH - 1 and g == 2) else (0, 1, 2, 3)
-                quant_and_multiply(j, g, order)
-                if g == 1:
-                    quant_and_multiply(j, 3, (0, 1, 2, 3))
+                quant(j, g)
+                if g == 0:
+                    quant(j, 3)
 
         def out_cols(j):
-            return out[:, :, CW * j : CW * (j + 1)].rearrange("b s n -> s b n")
+            return out[:, :, COL0[j] : COL0[j] + WIDTHS[j]].rearrange("b s n -> s b n")
 
-        def evacuate(j):
-            st = stgp.tile([P, MT, CW], F32, name="st", tag="st")
-            for mt in range(MT):
-                nc.scalar.copy(out=st[:, mt, :], in_=acc[j][mt][:])
-            nc.sync.dma_start(out=out_cols(j), in_=st[:])
+        def evacuate(j, last):
+            w = WIDTHS[j]
+            sa = stgp.tile([P, 2, CW], F32, name="sa", tag="st")
+            sb = stgp.tile([P, 2, CW], F32, name="sb", tag="st")
+            if last:
+                nc.scalar.copy(out=sa[:, 0, 0:w], in_=acc[j][0][:, 0:w])
+                nc.vector.tensor_copy(out=sb[:, 0, 0:w], in_=acc[j][2][:, 0:w])
+                nc.scalar.copy(out=sa[:, 1, 0:w], in_=acc[j][1][:, 0:w])
+                nc.vector.tensor_copy(out=sb[:, 1, 0:w], in_=acc[j][3][:, 0:w])
+                nc.sync.dma_start(out=out_cols(j)[:, 0:2, :], in_=sa[:, :, 0:w])
+                nc.sync.dma_start(out=out_cols(j)[:, 2:4, :], in_=sb[:, :, 0:w])
+            else:
+                nc.scalar.copy(out=sa[:, 0, 0:w], in_=acc[j][0][:, 0:w])
+                nc.scalar.copy(out=sa[:, 1, 0:w], in_=acc[j][1][:, 0:w])
+                nc.sync.dma_start(out=out_cols(j)[:, 0:2, :], in_=sa[:, :, 0:w])
+                nc.scalar.copy(out=sb[:, 0, 0:w], in_=acc[j][2][:, 0:w])
+                nc.scalar.copy(out=sb[:, 1, 0:w], in_=acc[j][3][:, 0:w])
+                nc.sync.dma_start(out=out_cols(j)[:, 2:4, :], in_=sb[:, :, 0:w])
 
-        for j in range(NCH):
+        scalar_units(0)
+        step(0)
+        step(1)
+        step(2)
+        for g in LOAD_ORDER:
+            load_w(g, (1,), rawu, "rawu")
+        for chunks in ((2, 3), (4, 5)):
+            for g in LOAD_ORDER:
+                load_w(g, chunks, raws, "raws")
+        for mt in range(MT):
+            transpose_x(mt)
+        vec_second(2)
+        quant(0, 1)
+        quant_x(0)
+        quant(0, 2)
+        quant_x(1)
+        quant_x(2)
+        quant_x(3)
+        x_ready[0] = True
+        for args in held:
+            multiply(*args)
+        scalar_units(1)
+        vec_first(3)
+        vec_first(4)
+        vec_second(3)
+        step(5)
+        evacuate(0, False)
+        for j in range(2, NCH):
             scalar_units(j)
             for n in (3 * j, 3 * j + 1, 3 * j + 2):
                 step(n)
             if j == 3:
-                for g in (0, 3, 1, 2):
-                    load_w(g, 3 * 2 * CW, 2 * CW, raws, "raws")
-            if j >= 1:
-                evacuate(j - 1)
+                for g in LOAD_ORDER:
+                    load_w(g, tuple(range(6, NCH)), raws, "raws")
+            evacuate(j - 1, False)
         step(NV)
         step(NV + 1)
-
-        j = NCH - 1
-        sa = stgp.tile([P, 2, CW], F32, name="sa", tag="st")
-        sb = stgp.tile([P, 2, CW], F32, name="sb", tag="st")
-        nc.scalar.copy(out=sa[:, 0, :], in_=acc[j][0][:])
-        nc.vector.tensor_copy(out=sb[:, 0, :], in_=acc[j][2][:])
-        nc.scalar.copy(out=sa[:, 1, :], in_=acc[j][1][:])
-        nc.vector.tensor_copy(out=sb[:, 1, :], in_=acc[j][3][:])
-        nc.sync.dma_start(out=out_cols(j)[:, 0:2, :], in_=sa[:])
-        nc.sync.dma_start(out=out_cols(j)[:, 2:4, :], in_=sb[:])
+        evacuate(NCH - 1, True)

@@ -18,16 +18,12 @@ P = 128
 CW = 512
 G = 4
 MT = 4
-INV = 1.0 / 0.6
+UP = 6.65625
+MASK = -0x3FFF4000
 WIDTHS = (512, 512, 512, 512, 512, 512, 512, 256, 256)
 NCH = 9
 COL0 = (0, 512, 1024, 1536, 2048, 2560, 3072, 3584, 3840)
-CS = 176
 LOAD_ORDER = (0, 3, 1, 2)
-
-
-def scalar_share(j):
-    return CS * WIDTHS[j] // CW
 
 
 def tile_ternarylinear_kernel(tc, x, kernel, out):
@@ -37,11 +33,9 @@ def tile_ternarylinear_kernel(tc, x, kernel, out):
         xgp = ctx.enter_context(tc.tile_pool(name="xgp", bufs=4))
         rawu = ctx.enter_context(tc.tile_pool(name="rawu", bufs=8))
         raws = ctx.enter_context(tc.tile_pool(name="raws", bufs=8))
-        tmpv = ctx.enter_context(tc.tile_pool(name="tmpv", bufs=2))
-        tmps = ctx.enter_context(tc.tile_pool(name="tmps", bufs=1))
         grpv = ctx.enter_context(tc.tile_pool(name="grpv", bufs=3))
-        grpm = ctx.enter_context(tc.tile_pool(name="grpm", bufs=2))
-        grps = ctx.enter_context(tc.tile_pool(name="grps", bufs=2))
+        grpm = ctx.enter_context(tc.tile_pool(name="grpm", bufs=5))
+        grps = ctx.enter_context(tc.tile_pool(name="grps", bufs=4))
         codp = ctx.enter_context(tc.tile_pool(name="codp", bufs=8))
         stgp = ctx.enter_context(tc.tile_pool(name="stgp", bufs=6))
         psum = ctx.enter_context(tc.psum_pool(name="psum", bufs=1))
@@ -90,63 +84,51 @@ def tile_ternarylinear_kernel(tc, x, kernel, out):
         def quant_x(mt):
             nc.vector.quantize_mx(out=xq[:, mt, :].bitcast(FP8X4), scales=xs[:, mt, :], in_=xg[mt][:])
 
-        grp = {}
-        tmp_of = {}
+        scaled = {}
+        tern = {}
         acc = {}
         held = []
         x_ready = [False]
         vunits = []
+        sunits = []
         for j in range(NCH):
-            vunits += [(j, 0, WIDTHS[j]), (j, 1, WIDTHS[j]), (j, 2, WIDTHS[j] - scalar_share(j))]
+            vunits += [(j, 0), (j, 1)]
+            sunits += [(j, 3), (j, 2)]
         NV = len(vunits)
 
-        def scalar_first(j, g, c0, ncols, tag):
+        def views(j, g, dst):
+            w = WIDTHS[j]
             rt, o = raw[(j, g)]
-            t = tmps.tile([P, 4, ncols], U32, name=tag, tag=tag)
-            nc.scalar.activation(out=t[:], in_=rt[:, :, o + c0 : o + c0 + ncols], func=ACT.Relu, bias=1.0, scale=INV)
-            return t
-
-        def scalar_second(t, gt, c0, ncols):
-            nc.scalar.activation(
-                out=gt[:, c0 : c0 + ncols, :].rearrange("p (c i) t -> p c t i", i=4),
-                in_=t[:].rearrange("p t (c i) -> p c t i", i=4),
-                func=ACT.Sign,
-                bias=-1.0,
-                scale=1.0,
+            return (
+                dst[:, 0:w, :].rearrange("p (c i) t -> p c t i", i=4),
+                rt[:, :, o : o + w].rearrange("p t (c i) -> p c t i", i=4),
             )
 
         def scalar_units(j):
+            for n in (2 * j, 2 * j + 1):
+                t = grps.tile([P, CW, 4], BF16, name="gs", tag="gs", align_bytes=64)
+                o, i = views(j, sunits[n][1], t)
+                nc.scalar.activation(out=o, in_=i, func=ACT.Copy, scale=UP)
+                scaled[sunits[n]] = t
+
+        def vec_scale(n):
+            j, g = vunits[n]
+            t = grpv.tile([P, CW, 4], BF16, name="gv", tag="gv", align_bytes=64)
+            o, i = views(j, g, t)
+            nc.vector.tensor_scalar(out=o, in0=i, scalar1=UP, scalar2=None, op0=ALU.mult)
+            scaled[(j, g)] = t
+
+        def vec_mask(j, g):
             w = WIDTHS[j]
-            cs = scalar_share(j)
-            t3 = scalar_first(j, 3, 0, w, "ts3")
-            t2 = scalar_first(j, 2, w - cs, cs, "ts2")
-            g3 = grps.tile([P, CW, 4], BF16, name="g3", tag="g3", align_bytes=64)
-            g2 = grpm.tile([P, CW, 4], BF16, name="g2", tag="g2", align_bytes=64)
-            grp[(j, 3)] = g3
-            grp[(j, 2)] = g2
-            scalar_second(t3, g3, 0, w)
-            scalar_second(t2, g2, w - cs, cs)
-
-        def vec_first(n):
-            j, g, ncols = vunits[n]
-            rt, o = raw[(j, g)]
-            t = tmpv.tile([P, 4, CW], I32, name="tv", tag="tv")
+            t = grpm.tile([P, 2 * CW], I32, name="gm", tag="gm", align_bytes=64)
             nc.vector.tensor_scalar(
-                out=t[:, :, 0:ncols], in0=rt[:, :, o : o + ncols], scalar1=INV, scalar2=-1.0, op0=ALU.mult, op1=ALU.max
-            )
-            tmp_of[n] = t
-
-        def vec_second(n):
-            j, g, ncols = vunits[n]
-            if g != 2:
-                grp[(j, g)] = grpv.tile([P, CW, 4], BF16, name="gv", tag="gv", align_bytes=64)
-            nc.vector.tensor_scalar(
-                out=grp[(j, g)][:, 0:ncols, :].rearrange("p (c i) t -> p c t i", i=4),
-                in0=tmp_of[n][:, :, 0:ncols].rearrange("p t (c i) -> p c t i", i=4),
-                scalar1=1.0,
+                out=t[:, 0 : 2 * w],
+                in0=scaled[(j, g)][:].rearrange("p c t -> p (c t)").bitcast(I32)[:, 0 : 2 * w],
+                scalar1=MASK,
                 scalar2=None,
-                op0=ALU.min,
+                op0=ALU.bitwise_and,
             )
+            tern[(j, g)] = t
 
         def multiply(j, g, cod, scl):
             w = WIDTHS[j]
@@ -172,7 +154,7 @@ def tile_ternarylinear_kernel(tc, x, kernel, out):
             cod = codp.tile([P, CW], U32, name="cod", tag="cod", align_bytes=64)
             scl = codp.tile([P, CW], U8, name="scl", tag="scl", align_bytes=64)
             nc.vector.quantize_mx(
-                out=cod[:, 0:w].bitcast(FP8X4), scales=scl[:, 0:w], in_=grp[(j, g)][:, 0:w, :].rearrange("p c t -> p (c t)")
+                out=cod[:, 0:w].bitcast(FP8X4), scales=scl[:, 0:w], in_=tern[(j, g)][:, 0 : 2 * w].bitcast(BF16)
             )
             if x_ready[0]:
                 multiply(j, g, cod, scl)
@@ -181,14 +163,13 @@ def tile_ternarylinear_kernel(tc, x, kernel, out):
 
         def step(n):
             if n < NV:
-                vec_first(n)
+                vec_scale(n)
             if 0 <= n - 1 < NV:
-                vec_second(n - 1)
+                vec_mask(*vunits[n - 1])
+                vec_mask(*sunits[n - 1])
             if 0 <= n - 2 < NV:
-                j, g, ncols = vunits[n - 2]
-                quant(j, g)
-                if g == 0:
-                    quant(j, 3)
+                quant(*vunits[n - 2])
+                quant(*sunits[n - 2])
 
         def out_cols(j):
             return out[:, :, COL0[j] : COL0[j] + WIDTHS[j]].rearrange("b s n -> s b n")
@@ -198,24 +179,23 @@ def tile_ternarylinear_kernel(tc, x, kernel, out):
             sa = stgp.tile([P, 2, CW], F32, name="sa", tag="st")
             sb = stgp.tile([P, 2, CW], F32, name="sb", tag="st")
             if last:
-                nc.scalar.copy(out=sa[:, 0, 0:w], in_=acc[j][0][:, 0:w])
-                nc.vector.tensor_copy(out=sb[:, 0, 0:w], in_=acc[j][2][:, 0:w])
-                nc.scalar.copy(out=sa[:, 1, 0:w], in_=acc[j][1][:, 0:w])
-                nc.vector.tensor_copy(out=sb[:, 1, 0:w], in_=acc[j][3][:, 0:w])
+                nc.scalar.activation(out=sa[:, 0, 0:w], in_=acc[j][0][:, 0:w], func=ACT.Copy, scale=0.5)
+                nc.vector.tensor_scalar(out=sb[:, 0, 0:w], in0=acc[j][2][:, 0:w], scalar1=0.5, scalar2=None, op0=ALU.mult)
+                nc.scalar.activation(out=sa[:, 1, 0:w], in_=acc[j][1][:, 0:w], func=ACT.Copy, scale=0.5)
+                nc.vector.tensor_scalar(out=sb[:, 1, 0:w], in0=acc[j][3][:, 0:w], scalar1=0.5, scalar2=None, op0=ALU.mult)
                 nc.sync.dma_start(out=out_cols(j)[:, 0:2, :], in_=sa[:, :, 0:w])
                 nc.sync.dma_start(out=out_cols(j)[:, 2:4, :], in_=sb[:, :, 0:w])
             else:
-                nc.scalar.copy(out=sa[:, 0, 0:w], in_=acc[j][0][:, 0:w])
-                nc.scalar.copy(out=sa[:, 1, 0:w], in_=acc[j][1][:, 0:w])
+                nc.scalar.activation(out=sa[:, 0, 0:w], in_=acc[j][0][:, 0:w], func=ACT.Copy, scale=0.5)
+                nc.scalar.activation(out=sa[:, 1, 0:w], in_=acc[j][1][:, 0:w], func=ACT.Copy, scale=0.5)
                 nc.sync.dma_start(out=out_cols(j)[:, 0:2, :], in_=sa[:, :, 0:w])
-                nc.scalar.copy(out=sb[:, 0, 0:w], in_=acc[j][2][:, 0:w])
-                nc.scalar.copy(out=sb[:, 1, 0:w], in_=acc[j][3][:, 0:w])
+                nc.scalar.activation(out=sb[:, 0, 0:w], in_=acc[j][2][:, 0:w], func=ACT.Copy, scale=0.5)
+                nc.scalar.activation(out=sb[:, 1, 0:w], in_=acc[j][3][:, 0:w], func=ACT.Copy, scale=0.5)
                 nc.sync.dma_start(out=out_cols(j)[:, 2:4, :], in_=sb[:, :, 0:w])
 
         scalar_units(0)
         step(0)
         step(1)
-        step(2)
         for g in LOAD_ORDER:
             load_w(g, (1,), rawu, "rawu")
         for chunks in ((2, 3), (4, 5)):
@@ -223,25 +203,28 @@ def tile_ternarylinear_kernel(tc, x, kernel, out):
                 load_w(g, chunks, raws, "raws")
         for mt in range(MT):
             transpose_x(mt)
-        vec_second(2)
-        quant(0, 1)
+        vec_mask(*vunits[1])
+        vec_mask(*sunits[1])
+        quant(*vunits[0])
+        quant(*sunits[0])
         quant_x(0)
-        quant(0, 2)
+        quant(*vunits[1])
         quant_x(1)
+        quant(*sunits[1])
         quant_x(2)
         quant_x(3)
         x_ready[0] = True
         for args in held:
             multiply(*args)
         scalar_units(1)
-        vec_first(3)
-        vec_first(4)
-        vec_second(3)
-        step(5)
+        vec_scale(2)
+        vec_scale(3)
+        vec_mask(*vunits[2])
+        vec_mask(*sunits[2])
         evacuate(0, False)
         for j in range(2, NCH):
             scalar_units(j)
-            for n in (3 * j, 3 * j + 1, 3 * j + 2):
+            for n in (2 * j, 2 * j + 1):
                 step(n)
             if j == 3:
                 for g in LOAD_ORDER:

@@ -31,13 +31,13 @@ def tile_ternarylinear_kernel(tc, x, kernel, out):
     with ExitStack() as ctx:
         const = ctx.enter_context(tc.tile_pool(name="const", bufs=1))
         xgp = ctx.enter_context(tc.tile_pool(name="xgp", bufs=4))
-        rawu = ctx.enter_context(tc.tile_pool(name="rawu", bufs=8))
+        rawu = ctx.enter_context(tc.tile_pool(name="rawu", bufs=12))
         raws = ctx.enter_context(tc.tile_pool(name="raws", bufs=8))
         grpv = ctx.enter_context(tc.tile_pool(name="grpv", bufs=3))
-        grpm = ctx.enter_context(tc.tile_pool(name="grpm", bufs=5))
+        grpm = ctx.enter_context(tc.tile_pool(name="grpm", bufs=4))
         grps = ctx.enter_context(tc.tile_pool(name="grps", bufs=4))
         codp = ctx.enter_context(tc.tile_pool(name="codp", bufs=8))
-        stgp = ctx.enter_context(tc.tile_pool(name="stgp", bufs=6))
+        stgp = ctx.enter_context(tc.tile_pool(name="stgp", bufs=5))
         psum = ctx.enter_context(tc.psum_pool(name="psum", bufs=1))
         ctx.enter_context(tc.manual_schedule())
 
@@ -66,6 +66,8 @@ def tile_ternarylinear_kernel(tc, x, kernel, out):
             t = rawu.tile([P, 2048], BF16, name="rawu", tag="rawu")
             nc.sync.dma_start(out=t[:], in_=x[mt])
             xr.append(t)
+        for g in LOAD_ORDER:
+            load_w(g, (1,), rawu, "rawu")
 
         xg = []
 
@@ -86,15 +88,11 @@ def tile_ternarylinear_kernel(tc, x, kernel, out):
 
         scaled = {}
         tern = {}
+        codes = {}
         acc = {}
+        done = {}
         held = []
         x_ready = [False]
-        vunits = []
-        sunits = []
-        for j in range(NCH):
-            vunits += [(j, 0), (j, 1)]
-            sunits += [(j, 3), (j, 2)]
-        NV = len(vunits)
 
         def views(j, g, dst):
             w = WIDTHS[j]
@@ -104,15 +102,15 @@ def tile_ternarylinear_kernel(tc, x, kernel, out):
                 rt[:, :, o : o + w].rearrange("p t (c i) -> p c t i", i=4),
             )
 
-        def scalar_units(j):
-            for n in (2 * j, 2 * j + 1):
-                t = grps.tile([P, CW, 4], BF16, name="gs", tag="gs", align_bytes=64)
-                o, i = views(j, sunits[n][1], t)
-                nc.scalar.activation(out=o, in_=i, func=ACT.Copy, scale=UP)
-                scaled[sunits[n]] = t
+        def scalar_scale(j, g):
+            if j >= NCH:
+                return
+            t = grps.tile([P, CW, 4], BF16, name="gs", tag="gs", align_bytes=64)
+            o, i = views(j, g, t)
+            nc.scalar.activation(out=o, in_=i, func=ACT.Copy, scale=UP)
+            scaled[(j, g)] = t
 
-        def vec_scale(n):
-            j, g = vunits[n]
+        def vec_scale(j, g):
             t = grpv.tile([P, CW, 4], BF16, name="gv", tag="gv", align_bytes=64)
             o, i = views(j, g, t)
             nc.vector.tensor_scalar(out=o, in0=i, scalar1=UP, scalar2=None, op0=ALU.mult)
@@ -130,25 +128,6 @@ def tile_ternarylinear_kernel(tc, x, kernel, out):
             )
             tern[(j, g)] = t
 
-        def multiply(j, g, cod, scl):
-            w = WIDTHS[j]
-            if g == 0:
-                acc[j] = [
-                    psum.tile([P, CW], F32, name="acc%d" % (4 * (j % 2) + mt), tag="bank%d" % (4 * (j % 2) + mt))
-                    for mt in range(MT)
-                ]
-            order = (0, 2, 1, 3) if (j == NCH - 1 and g == 2) else (0, 1, 2, 3)
-            for mt in order:
-                nc.tensor.matmul_mx(
-                    out=acc[j][mt][:, 0:w],
-                    lhsT=xq[:, mt, P * g : P * (g + 1)].bitcast(FP8X4),
-                    lhsT_scale=xs[:, mt, P * g : P * (g + 1)],
-                    rhs=cod[:, 0:w].bitcast(FP8X4),
-                    rhs_scale=scl[:, 0:w],
-                    start=(g == 0),
-                    stop=(g == 2),
-                )
-
         def quant(j, g):
             w = WIDTHS[j]
             cod = codp.tile([P, CW], U32, name="cod", tag="cod", align_bytes=64)
@@ -156,80 +135,104 @@ def tile_ternarylinear_kernel(tc, x, kernel, out):
             nc.vector.quantize_mx(
                 out=cod[:, 0:w].bitcast(FP8X4), scales=scl[:, 0:w], in_=tern[(j, g)][:, 0 : 2 * w].bitcast(BF16)
             )
+            codes[(j, g)] = (cod, scl)
             if x_ready[0]:
-                multiply(j, g, cod, scl)
+                passes(j, g)
             else:
-                held.append((j, g, cod, scl))
+                held.append((j, g))
 
-        def step(n):
-            if n < NV:
-                vec_scale(n)
-            if 0 <= n - 1 < NV:
-                vec_mask(*vunits[n - 1])
-                vec_mask(*sunits[n - 1])
-            if 0 <= n - 2 < NV:
-                quant(*vunits[n - 2])
-                quant(*sunits[n - 2])
+
+        def passes(j, g):
+            w = WIDTHS[j]
+            cod, scl = codes[(j, g)]
+            done[j] = done.get(j, 0) + 1
+            if done[j] == 1:
+                acc[j] = [
+                    psum.tile([P, CW], F32, name="acc%d" % (4 * (j % 2) + mt), tag="bank%d" % (4 * (j % 2) + mt))
+                    for mt in range(MT)
+                ]
+            for mt in (0, 2, 1, 3):
+                nc.tensor.matmul_mx(
+                    out=acc[j][mt][:, 0:w],
+                    lhsT=xq[:, mt, P * g : P * (g + 1)].bitcast(FP8X4),
+                    lhsT_scale=xs[:, mt, P * g : P * (g + 1)],
+                    rhs=cod[:, 0:w].bitcast(FP8X4),
+                    rhs_scale=scl[:, 0:w],
+                    start=(done[j] == 1),
+                    stop=(done[j] == G),
+                )
 
         def out_cols(j):
             return out[:, :, COL0[j] : COL0[j] + WIDTHS[j]].rearrange("b s n -> s b n")
 
-        def evacuate(j, last):
+        def evac_scalar(j, half):
             w = WIDTHS[j]
-            sa = stgp.tile([P, 2, CW], F32, name="sa", tag="st")
-            sb = stgp.tile([P, 2, CW], F32, name="sb", tag="st")
-            if last:
-                nc.scalar.activation(out=sa[:, 0, 0:w], in_=acc[j][0][:, 0:w], func=ACT.Copy, scale=0.5)
-                nc.vector.tensor_scalar(out=sb[:, 0, 0:w], in0=acc[j][2][:, 0:w], scalar1=0.5, scalar2=None, op0=ALU.mult)
-                nc.scalar.activation(out=sa[:, 1, 0:w], in_=acc[j][1][:, 0:w], func=ACT.Copy, scale=0.5)
-                nc.vector.tensor_scalar(out=sb[:, 1, 0:w], in0=acc[j][3][:, 0:w], scalar1=0.5, scalar2=None, op0=ALU.mult)
-                nc.sync.dma_start(out=out_cols(j)[:, 0:2, :], in_=sa[:, :, 0:w])
-                nc.sync.dma_start(out=out_cols(j)[:, 2:4, :], in_=sb[:, :, 0:w])
-            else:
-                nc.scalar.activation(out=sa[:, 0, 0:w], in_=acc[j][0][:, 0:w], func=ACT.Copy, scale=0.5)
-                nc.scalar.activation(out=sa[:, 1, 0:w], in_=acc[j][1][:, 0:w], func=ACT.Copy, scale=0.5)
-                nc.sync.dma_start(out=out_cols(j)[:, 0:2, :], in_=sa[:, :, 0:w])
-                nc.scalar.activation(out=sb[:, 0, 0:w], in_=acc[j][2][:, 0:w], func=ACT.Copy, scale=0.5)
-                nc.scalar.activation(out=sb[:, 1, 0:w], in_=acc[j][3][:, 0:w], func=ACT.Copy, scale=0.5)
-                nc.sync.dma_start(out=out_cols(j)[:, 2:4, :], in_=sb[:, :, 0:w])
+            st = stgp.tile([P, 2, CW], F32, name="st", tag="st")
+            for u in range(2):
+                nc.scalar.activation(out=st[:, u, 0:w], in_=acc[j][2 * half + u][:, 0:w], func=ACT.Copy, scale=0.5)
+            nc.sync.dma_start(out=out_cols(j)[:, 2 * half : 2 * half + 2, :], in_=st[:, :, 0:w])
 
-        scalar_units(0)
-        step(0)
-        step(1)
+        def vec_tail(j):
+            vec_mask(j, 3)
+            vec_scale(j, 1)
+            vec_mask(j, 0)
+            quant(j, 3)
+            vec_mask(j, 2)
+            quant(j, 0)
+            vec_mask(j, 1)
+            quant(j, 2)
+
+        def evac_last(j):
+            w = WIDTHS[j]
+            st = []
+            for half in range(2):
+                t = stgp.tile([P, 2, CW], F32, name="st", tag="st")
+                st.append(t)
+            for u in range(2):
+                nc.scalar.activation(out=st[0][:, u, 0:w], in_=acc[j][u][:, 0:w], func=ACT.Copy, scale=0.5)
+                nc.vector.tensor_scalar(
+                    out=st[1][:, u, 0:w], in0=acc[j][2 + u][:, 0:w], scalar1=0.5, scalar2=None, op0=ALU.mult
+                )
+            for half in range(2):
+                nc.sync.dma_start(out=out_cols(j)[:, 2 * half : 2 * half + 2, :], in_=st[half][:, :, 0:w])
+
+        scalar_scale(0, 3)
+        scalar_scale(0, 2)
+        vec_scale(0, 0)
+        vec_scale(0, 1)
         for g in LOAD_ORDER:
-            load_w(g, (1,), rawu, "rawu")
-        for chunks in ((2, 3), (4, 5)):
+            load_w(g, (2,), rawu, "rawu")
+        for chunks in ((3, 4), (5, 6)):
             for g in LOAD_ORDER:
                 load_w(g, chunks, raws, "raws")
+        vec_mask(0, 0)
+        vec_mask(0, 3)
+        quant(0, 0)
+        vec_mask(0, 1)
+        quant(0, 3)
+        vec_mask(0, 2)
+        quant(0, 1)
         for mt in range(MT):
             transpose_x(mt)
-        vec_mask(*vunits[1])
-        vec_mask(*sunits[1])
-        quant(*vunits[0])
-        quant(*sunits[0])
-        quant_x(0)
-        quant(*vunits[1])
-        quant_x(1)
-        quant(*sunits[1])
-        quant_x(2)
-        quant_x(3)
-        x_ready[0] = True
-        for args in held:
-            multiply(*args)
-        scalar_units(1)
-        vec_scale(2)
-        vec_scale(3)
-        vec_mask(*vunits[2])
-        vec_mask(*sunits[2])
-        evacuate(0, False)
-        for j in range(2, NCH):
-            scalar_units(j)
-            for n in (2 * j, 2 * j + 1):
-                step(n)
-            if j == 3:
+        scalar_scale(1, 3)
+        scalar_scale(1, 2)
+        for j in range(1, NCH):
+            scalar_scale(j + 1, 3)
+            scalar_scale(j + 1, 2)
+            vec_scale(j, 0)
+            quant(j - 1, 2 if j == 1 else 1)
+            if j == 1:
+                for mt in range(MT):
+                    quant_x(mt)
+                x_ready[0] = True
+                for args in held:
+                    passes(*args)
+            vec_tail(j)
+            evac_scalar(j - 1, 0)
+            evac_scalar(j - 1, 1)
+            if j == 2:
                 for g in LOAD_ORDER:
-                    load_w(g, tuple(range(6, NCH)), raws, "raws")
-            evacuate(j - 1, False)
-        step(NV)
-        step(NV + 1)
-        evacuate(NCH - 1, True)
+                    load_w(g, (7, 8), rawu, "rawu")
+        last = NCH - 1
+        quant(last, 1)
+        evac_last(last)

@@ -98,8 +98,8 @@ def tile_ternarylinear_kernel(tc, x, kernel, out):
             w = WIDTHS[j]
             rt, o = raw[(j, g)]
             return (
-                dst[:, 0:w, :].rearrange("p (c i) t -> p c t i", i=4),
-                rt[:, :, o : o + w].rearrange("p t (c i) -> p c t i", i=4),
+                dst[:, 0:w, :].rearrange("p (c i) t -> p c t i", i=8),
+                rt[:, :, o : o + w].rearrange("p t (c i) -> p c t i", i=8),
             )
 
         def scalar_scale(j, g):

@@ -23,21 +23,21 @@ MASK = -0x3FFF4000
 WIDTHS = (512, 512, 512, 512, 512, 512, 512, 256, 256)
 NCH = 9
 COL0 = (0, 512, 1024, 1536, 2048, 2560, 3072, 3584, 3840)
-LOAD_ORDER = (0, 3, 1, 2)
+CSH = 0
 
 
 def tile_ternarylinear_kernel(tc, x, kernel, out):
     nc = tc.nc
     with ExitStack() as ctx:
         const = ctx.enter_context(tc.tile_pool(name="const", bufs=1))
-        xgp = ctx.enter_context(tc.tile_pool(name="xgp", bufs=4))
-        rawu = ctx.enter_context(tc.tile_pool(name="rawu", bufs=12))
+        xgp = ctx.enter_context(tc.tile_pool(name="xgp", bufs=3))
+        rawu = ctx.enter_context(tc.tile_pool(name="rawu", bufs=8))
         raws = ctx.enter_context(tc.tile_pool(name="raws", bufs=8))
-        grpv = ctx.enter_context(tc.tile_pool(name="grpv", bufs=3))
-        grpm = ctx.enter_context(tc.tile_pool(name="grpm", bufs=4))
-        grps = ctx.enter_context(tc.tile_pool(name="grps", bufs=4))
-        codp = ctx.enter_context(tc.tile_pool(name="codp", bufs=8))
-        stgp = ctx.enter_context(tc.tile_pool(name="stgp", bufs=5))
+        grpv = ctx.enter_context(tc.tile_pool(name="grpv", bufs=2))
+        grpm = ctx.enter_context(tc.tile_pool(name="grpm", bufs=2))
+        grps = ctx.enter_context(tc.tile_pool(name="grps", bufs=3))
+        codp = ctx.enter_context(tc.tile_pool(name="codp", bufs=6))
+        stgp = ctx.enter_context(tc.tile_pool(name="stgp", bufs=7))
         psum = ctx.enter_context(tc.psum_pool(name="psum", bufs=1))
         ctx.enter_context(tc.manual_schedule())
 
@@ -59,15 +59,17 @@ def tile_ternarylinear_kernel(tc, x, kernel, out):
             for j in chunks:
                 raw[(j, g)] = (t, COL0[j] - c0)
 
-        for g in LOAD_ORDER:
-            load_w(g, (0,), rawu, "rawu")
+        load_w(0, (0,), rawu, "rawu")
         xr = []
         for mt in range(MT):
             t = rawu.tile([P, 2048], BF16, name="rawu", tag="rawu")
             nc.sync.dma_start(out=t[:], in_=x[mt])
             xr.append(t)
-        for g in LOAD_ORDER:
-            load_w(g, (1,), rawu, "rawu")
+        for g in (3, 1, 2):
+            load_w(g, (0,), rawu, "rawu")
+        for chunks, order in (((1, 2), (3, 0, 2, 1)), ((3, 4), (3, 2, 0, 1))):
+            for g in order:
+                load_w(g, chunks, raws, "raws")
 
         xg = []
 
@@ -86,153 +88,200 @@ def tile_ternarylinear_kernel(tc, x, kernel, out):
         def quant_x(mt):
             nc.vector.quantize_mx(out=xq[:, mt, :].bitcast(FP8X4), scales=xs[:, mt, :], in_=xg[mt][:])
 
-        scaled = {}
-        tern = {}
-        codes = {}
+        home = {}
         acc = {}
         done = {}
-        held = []
-        x_ready = [False]
 
-        def views(j, g, dst):
-            w = WIDTHS[j]
+        def place(pool, tag, units):
+            t = pool.tile([P, 2 * CW, 4], BF16, name=tag, tag=tag, align_bytes=64)
+            c = 0
+            for j, g in units:
+                home[(j, g)] = (t, c)
+                c += WIDTHS[j]
+
+        def views(j, g, c0, c1):
+            t, h = home[(j, g)]
             rt, o = raw[(j, g)]
             return (
-                dst[:, 0:w, :].rearrange("p (c i) t -> p c t i", i=8),
-                rt[:, :, o : o + w].rearrange("p t (c i) -> p c t i", i=8),
+                t[:, h + c0 : h + c1, :].rearrange("p (c i) t -> p c t i", i=4),
+                rt[:, :, o + c0 : o + c1].rearrange("p t (c i) -> p c t i", i=4),
             )
 
-        def scalar_scale(j, g):
-            if j >= NCH:
-                return
-            t = grps.tile([P, CW, 4], BF16, name="gs", tag="gs", align_bytes=64)
-            o, i = views(j, g, t)
+        def scalar_scale(j, g, c0, c1):
+            o, i = views(j, g, c0, c1)
             nc.scalar.activation(out=o, in_=i, func=ACT.Copy, scale=UP)
-            scaled[(j, g)] = t
 
-        def vec_scale(j, g):
-            t = grpv.tile([P, CW, 4], BF16, name="gv", tag="gv", align_bytes=64)
-            o, i = views(j, g, t)
+        def vec_scale(j, g, c0, c1):
+            o, i = views(j, g, c0, c1)
             nc.vector.tensor_scalar(out=o, in0=i, scalar1=UP, scalar2=None, op0=ALU.mult)
-            scaled[(j, g)] = t
 
-        def vec_mask(j, g):
-            w = WIDTHS[j]
-            t = grpm.tile([P, 2 * CW], I32, name="gm", tag="gm", align_bytes=64)
+        tern = {}
+        codes = {}
+
+        def columns(units):
+            return sum(WIDTHS[j] for j, g in units)
+
+        def vec_mask(units):
+            w = columns(units)
+            t = grpm.tile([P, 4 * CW], I32, name="gm", tag="gm", align_bytes=64)
             nc.vector.tensor_scalar(
                 out=t[:, 0 : 2 * w],
-                in0=scaled[(j, g)][:].rearrange("p c t -> p (c t)").bitcast(I32)[:, 0 : 2 * w],
+                in0=home[units[0]][0][:].rearrange("p c t -> p (c t)").bitcast(I32)[:, 0 : 2 * w],
                 scalar1=MASK,
                 scalar2=None,
                 op0=ALU.bitwise_and,
             )
-            tern[(j, g)] = t
+            tern[units] = t
 
-        def quant(j, g):
-            w = WIDTHS[j]
-            cod = codp.tile([P, CW], U32, name="cod", tag="cod", align_bytes=64)
-            scl = codp.tile([P, CW], U8, name="scl", tag="scl", align_bytes=64)
+        def quant(units):
+            w = columns(units)
+            cod = codp.tile([P, 2 * CW], U32, name="cod", tag="cod", align_bytes=64)
+            scl = codp.tile([P, 2 * CW], U8, name="scl", tag="scl", align_bytes=64)
             nc.vector.quantize_mx(
-                out=cod[:, 0:w].bitcast(FP8X4), scales=scl[:, 0:w], in_=tern[(j, g)][:, 0 : 2 * w].bitcast(BF16)
+                out=cod[:, 0:w].bitcast(FP8X4), scales=scl[:, 0:w], in_=tern[units][:, 0 : 2 * w].bitcast(BF16)
             )
-            codes[(j, g)] = (cod, scl)
-            if x_ready[0]:
-                passes(j, g)
-            else:
-                held.append((j, g))
+            codes[units] = (cod, scl)
 
+        def passes(units, chunks):
+            cod, scl = codes[units]
+            for j, g in units:
+                if j not in chunks:
+                    continue
+                w = WIDTHS[j]
+                c = home[(j, g)][1]
+                done[j] = done.get(j, 0) + 1
+                if done[j] == 1:
+                    acc[j] = []
+                    for mt in range(MT):
+                        k = (MT * j + mt) % 8
+                        bank = psum.tile([P, CW], F32, name="acc%d" % k, tag="bank%d" % k)
+                        acc[j].append(bank)
+                for mt in range(MT):
+                    nc.tensor.matmul_mx(
+                        out=acc[j][mt][:, 0:w],
+                        lhsT=xq[:, mt, P * g : P * (g + 1)].bitcast(FP8X4),
+                        lhsT_scale=xs[:, mt, P * g : P * (g + 1)],
+                        rhs=cod[:, c : c + w].bitcast(FP8X4),
+                        rhs_scale=scl[:, c : c + w],
+                        start=(done[j] == 1),
+                        stop=(done[j] == G),
+                    )
 
-        def passes(j, g):
-            w = WIDTHS[j]
-            cod, scl = codes[(j, g)]
-            done[j] = done.get(j, 0) + 1
-            if done[j] == 1:
-                acc[j] = [
-                    psum.tile([P, CW], F32, name="acc%d" % (4 * (j % 2) + mt), tag="bank%d" % (4 * (j % 2) + mt))
-                    for mt in range(MT)
-                ]
-            for mt in (0, 2, 1, 3):
-                nc.tensor.matmul_mx(
-                    out=acc[j][mt][:, 0:w],
-                    lhsT=xq[:, mt, P * g : P * (g + 1)].bitcast(FP8X4),
-                    lhsT_scale=xs[:, mt, P * g : P * (g + 1)],
-                    rhs=cod[:, 0:w].bitcast(FP8X4),
-                    rhs_scale=scl[:, 0:w],
-                    start=(done[j] == 1),
-                    stop=(done[j] == G),
-                )
-
-        def out_cols(j):
-            return out[:, :, COL0[j] : COL0[j] + WIDTHS[j]].rearrange("b s n -> s b n")
-
-        def evac_scalar(j, half):
+        def evac_half(j, half, engine):
             w = WIDTHS[j]
             st = stgp.tile([P, 2, CW], F32, name="st", tag="st")
             for u in range(2):
-                nc.scalar.activation(out=st[:, u, 0:w], in_=acc[j][2 * half + u][:, 0:w], func=ACT.Copy, scale=0.5)
-            nc.sync.dma_start(out=out_cols(j)[:, 2 * half : 2 * half + 2, :], in_=st[:, :, 0:w])
+                if engine == "vector":
+                    nc.vector.tensor_scalar(
+                        out=st[:, u, 0:w], in0=acc[j][2 * half + u][:, 0:w], scalar1=0.5, scalar2=None, op0=ALU.mult
+                    )
+                else:
+                    nc.scalar.activation(out=st[:, u, 0:w], in_=acc[j][2 * half + u][:, 0:w], func=ACT.Copy, scale=0.5)
+            nc.sync.dma_start(
+                out=out[2 * half : 2 * half + 2, :, COL0[j] : COL0[j] + w].rearrange("b s n -> s b n"), in_=st[:, :, 0:w]
+            )
 
-        def vec_tail(j):
-            vec_mask(j, 3)
-            vec_scale(j, 1)
-            vec_mask(j, 0)
-            quant(j, 3)
-            vec_mask(j, 2)
-            quant(j, 0)
-            vec_mask(j, 1)
-            quant(j, 2)
+        def evac(j):
+            evac_half(j, 0, "scalar")
+            evac_half(j, 1, "scalar")
 
-        def evac_last(j):
-            w = WIDTHS[j]
-            st = []
-            for half in range(2):
-                t = stgp.tile([P, 2, CW], F32, name="st", tag="st")
-                st.append(t)
-            for u in range(2):
-                nc.scalar.activation(out=st[0][:, u, 0:w], in_=acc[j][u][:, 0:w], func=ACT.Copy, scale=0.5)
-                nc.vector.tensor_scalar(
-                    out=st[1][:, u, 0:w], in0=acc[j][2 + u][:, 0:w], scalar1=0.5, scalar2=None, op0=ALU.mult
-                )
-            for half in range(2):
-                nc.sync.dma_start(out=out_cols(j)[:, 2 * half : 2 * half + 2, :], in_=st[half][:, :, 0:w])
+        def alone(g):
+            return ((0, g),)
 
-        scalar_scale(0, 3)
-        scalar_scale(0, 2)
-        vec_scale(0, 0)
-        vec_scale(0, 1)
-        for g in LOAD_ORDER:
-            load_w(g, (2,), rawu, "rawu")
-        for chunks in ((3, 4), (5, 6)):
-            for g in LOAD_ORDER:
-                load_w(g, chunks, raws, "raws")
-        vec_mask(0, 0)
-        vec_mask(0, 3)
-        quant(0, 0)
-        vec_mask(0, 1)
-        quant(0, 3)
-        vec_mask(0, 2)
-        quant(0, 1)
+        for g in range(G):
+            place(grpv if g < 2 else grps, "gv" if g < 2 else "gs", alone(g))
+        vec_scale(0, 0, 0, CW)
+        vec_mask(alone(0))
+        quant(alone(0))
         for mt in range(MT):
             transpose_x(mt)
-        scalar_scale(1, 3)
-        scalar_scale(1, 2)
-        for j in range(1, NCH):
-            scalar_scale(j + 1, 3)
-            scalar_scale(j + 1, 2)
-            vec_scale(j, 0)
-            quant(j - 1, 2 if j == 1 else 1)
-            if j == 1:
-                for mt in range(MT):
-                    quant_x(mt)
-                x_ready[0] = True
-                for args in held:
-                    passes(*args)
-            vec_tail(j)
-            evac_scalar(j - 1, 0)
-            evac_scalar(j - 1, 1)
-            if j == 2:
-                for g in LOAD_ORDER:
+        scalar_scale(0, 3, 0, CW)
+        scalar_scale(0, 2, 0, CW)
+        for mt in range(MT):
+            quant_x(mt)
+        passes(alone(0), (0,))
+        vec_scale(0, 1, 0, CW)
+        vec_mask(alone(3))
+        quant(alone(3))
+        passes(alone(3), (0,))
+        vec_mask(alone(1))
+        quant(alone(1))
+        passes(alone(1), (0,))
+
+        def pair(g):
+            return ((1, g), (2, g))
+
+        place(grps, "gs", pair(3))
+        for j, g in pair(3):
+            scalar_scale(j, g, 0, CW)
+        place(grpv, "gv", pair(0))
+        vec_mask(alone(2))
+        for j, g in pair(0):
+            vec_scale(j, g, 0, CW)
+        quant(alone(2))
+        passes(alone(2), (0,))
+        vec_mask(pair(3))
+        place(grps, "gs", pair(2))
+        for j, g in pair(2):
+            scalar_scale(j, g, 0, CW)
+        evac(0)
+        vec_mask(pair(0))
+        quant(pair(3))
+        passes(pair(3), (1,))
+        place(grpv, "gv", pair(1))
+        vec_scale(1, 1, 0, CW)
+        quant(pair(0))
+        passes(pair(0), (1,))
+        vec_scale(2, 1, 0, CW)
+
+        def by_scalar(j):
+            return ((j, 3), (j, 2))
+
+        def by_vector(j):
+            return ((j, 0), (j, 1))
+
+        def share(j):
+            return CSH * WIDTHS[j] // CW
+
+        def ahead_scalar(j):
+            if j >= NCH:
+                return
+            place(grps, "gs", by_scalar(j))
+            place(grpv, "gv", by_vector(j))
+            scalar_scale(j, 3, 0, WIDTHS[j])
+            scalar_scale(j, 2, 0, WIDTHS[j])
+            if share(j):
+                scalar_scale(j, 1, 0, share(j))
+
+        ahead_scalar(3)
+        vec_mask(pair(2))
+        vec_mask(pair(1))
+        quant(pair(2))
+        passes(pair(2), (1,))
+        for j in range(3, NCH):
+            vec_scale(j, 0, 0, WIDTHS[j])
+            if j == 3:
+                quant(pair(1))
+                passes(pair(1), (1,))
+                for g in (3, 0, 2, 1):
+                    passes(pair(g), (2,))
+                for g in (3, 2, 0, 1):
+                    load_w(g, (5, 6), raws, "raws")
+            else:
+                quant(by_vector(j - 1))
+                passes(by_vector(j - 1), (j - 1,))
+            ahead_scalar(j + 1)
+            evac(j - 2)
+            if j == 4:
+                for g in (3, 2, 0, 1):
                     load_w(g, (7, 8), rawu, "rawu")
-        last = NCH - 1
-        quant(last, 1)
-        evac_last(last)
+            vec_mask(by_scalar(j))
+            vec_scale(j, 1, share(j), WIDTHS[j])
+            quant(by_scalar(j))
+            passes(by_scalar(j), (j,))
+            vec_mask(by_vector(j))
+        quant(by_vector(NCH - 1))
+        passes(by_vector(NCH - 1), (NCH - 1,))
+        evac(NCH - 2)
+        evac_half(NCH - 1, 0, "scalar")
+        evac_half(NCH - 1, 1, "vector")

@@ -23,21 +23,21 @@ MASK = -0x3FFF4000
 WIDTHS = (512, 512, 512, 512, 512, 512, 512, 256, 256)
 NCH = 9
 COL0 = (0, 512, 1024, 1536, 2048, 2560, 3072, 3584, 3840)
-CSH = 0
+HELPED = (3,)
+CSH = 64
 
 
 def tile_ternarylinear_kernel(tc, x, kernel, out):
     nc = tc.nc
     with ExitStack() as ctx:
         const = ctx.enter_context(tc.tile_pool(name="const", bufs=1))
-        xgp = ctx.enter_context(tc.tile_pool(name="xgp", bufs=3))
         rawu = ctx.enter_context(tc.tile_pool(name="rawu", bufs=8))
         raws = ctx.enter_context(tc.tile_pool(name="raws", bufs=8))
-        grpv = ctx.enter_context(tc.tile_pool(name="grpv", bufs=2))
+        grpv = ctx.enter_context(tc.tile_pool(name="grpv", bufs=3))
         grpm = ctx.enter_context(tc.tile_pool(name="grpm", bufs=2))
         grps = ctx.enter_context(tc.tile_pool(name="grps", bufs=3))
         codp = ctx.enter_context(tc.tile_pool(name="codp", bufs=6))
-        stgp = ctx.enter_context(tc.tile_pool(name="stgp", bufs=7))
+        stgp = ctx.enter_context(tc.tile_pool(name="stgp", bufs=8))
         psum = ctx.enter_context(tc.psum_pool(name="psum", bufs=1))
         ctx.enter_context(tc.manual_schedule())
 
@@ -59,23 +59,25 @@ def tile_ternarylinear_kernel(tc, x, kernel, out):
             for j in chunks:
                 raw[(j, g)] = (t, COL0[j] - c0)
 
-        load_w(0, (0,), rawu, "rawu")
+        for g in (0, 3, 1, 2):
+            load_w(g, (0,), rawu, "rawu")
+        for g in (3, 0):
+            load_w(g, (1, 2), raws, "raws")
         xr = []
         for mt in range(MT):
             t = rawu.tile([P, 2048], BF16, name="rawu", tag="rawu")
             nc.sync.dma_start(out=t[:], in_=x[mt])
             xr.append(t)
-        for g in (3, 1, 2):
-            load_w(g, (0,), rawu, "rawu")
-        for chunks, order in (((1, 2), (3, 0, 2, 1)), ((3, 4), (3, 2, 0, 1))):
-            for g in order:
-                load_w(g, chunks, raws, "raws")
+        for g in (2, 1):
+            load_w(g, (1, 2), raws, "raws")
+        for g in (3, 0, 2, 1):
+            load_w(g, (3, 4), raws, "raws")
 
         xg = []
 
         def transpose_x(mt):
             xw = xr[mt][:].bitcast(F32).rearrange("p (g w u) -> p g u w", g=G, u=2)
-            xgt = xgp.tile([P, 2048], BF16, name="xg", tag="xg", align_bytes=64)
+            xgt = stgp.tile([P, 2048], BF16, name="st", tag="st", align_bytes=64)
             xg.append(xgt)
             for h in range(2):
                 bank = psum.tile([P, 4, P], F32, name="xb%d" % (2 * mt + h), tag="bank%d" % (2 * mt + h))
@@ -123,10 +125,11 @@ def tile_ternarylinear_kernel(tc, x, kernel, out):
 
         def vec_mask(units):
             w = columns(units)
+            t0, c0 = home[units[0]]
             t = grpm.tile([P, 4 * CW], I32, name="gm", tag="gm", align_bytes=64)
             nc.vector.tensor_scalar(
                 out=t[:, 0 : 2 * w],
-                in0=home[units[0]][0][:].rearrange("p c t -> p (c t)").bitcast(I32)[:, 0 : 2 * w],
+                in0=t0[:].rearrange("p c t -> p (c t)").bitcast(I32)[:, 2 * c0 : 2 * (c0 + w)],
                 scalar1=MASK,
                 scalar2=None,
                 op0=ALU.bitwise_and,
@@ -148,7 +151,7 @@ def tile_ternarylinear_kernel(tc, x, kernel, out):
                 if j not in chunks:
                     continue
                 w = WIDTHS[j]
-                c = home[(j, g)][1]
+                c = home[(j, g)][1] - home[units[0]][1]
                 done[j] = done.get(j, 0) + 1
                 if done[j] == 1:
                     acc[j] = []
@@ -169,7 +172,7 @@ def tile_ternarylinear_kernel(tc, x, kernel, out):
 
         def evac_half(j, half, engine):
             w = WIDTHS[j]
-            st = stgp.tile([P, 2, CW], F32, name="st", tag="st")
+            st = stgp.tile([P, 2, CW], F32, name="st", tag="st", align_bytes=64)
             for u in range(2):
                 if engine == "vector":
                     nc.vector.tensor_scalar(
@@ -181,6 +184,17 @@ def tile_ternarylinear_kernel(tc, x, kernel, out):
                 out=out[2 * half : 2 * half + 2, :, COL0[j] : COL0[j] + w].rearrange("b s n -> s b n"), in_=st[:, :, 0:w]
             )
 
+        def evac_one(j, mt, engine):
+            w = WIDTHS[j]
+            st = stgp.tile([P, 2, CW], F32, name="st", tag="st", align_bytes=64)
+            if engine == "vector":
+                nc.vector.tensor_scalar(
+                    out=st[:, 0, 0:w], in0=acc[j][mt][:, 0:w], scalar1=0.5, scalar2=None, op0=ALU.mult
+                )
+            else:
+                nc.scalar.activation(out=st[:, 0, 0:w], in_=acc[j][mt][:, 0:w], func=ACT.Copy, scale=0.5)
+            nc.sync.dma_start(out=out[mt, :, COL0[j] : COL0[j] + w], in_=st[:, 0, 0:w])
+
         def evac(j):
             evac_half(j, 0, "scalar")
             evac_half(j, 1, "scalar")
@@ -190,48 +204,45 @@ def tile_ternarylinear_kernel(tc, x, kernel, out):
 
         for g in range(G):
             place(grpv if g < 2 else grps, "gv" if g < 2 else "gs", alone(g))
-        vec_scale(0, 0, 0, CW)
-        vec_mask(alone(0))
-        quant(alone(0))
-        for mt in range(MT):
-            transpose_x(mt)
-        scalar_scale(0, 3, 0, CW)
-        scalar_scale(0, 2, 0, CW)
-        for mt in range(MT):
-            quant_x(mt)
-        passes(alone(0), (0,))
-        vec_scale(0, 1, 0, CW)
-        vec_mask(alone(3))
-        quant(alone(3))
-        passes(alone(3), (0,))
-        vec_mask(alone(1))
-        quant(alone(1))
-        passes(alone(1), (0,))
-
         def pair(g):
             return ((1, g), (2, g))
 
+        vec_scale(0, 0, 0, CW)
+        scalar_scale(0, 3, 0, CW)
+        vec_scale(0, 1, 0, CW)
+        vec_mask(alone(0))
+        scalar_scale(0, 2, 0, CW)
+        vec_mask(alone(1))
+        quant(alone(0))
+        vec_mask(alone(3))
+        quant(alone(1))
         place(grps, "gs", pair(3))
         for j, g in pair(3):
             scalar_scale(j, g, 0, CW)
-        place(grpv, "gv", pair(0))
+        for mt in range(MT):
+            transpose_x(mt)
         vec_mask(alone(2))
-        for j, g in pair(0):
-            vec_scale(j, g, 0, CW)
+        quant(alone(3))
+        place(grpv, "gv", pair(0))
+        vec_scale(1, 0, 0, CW)
         quant(alone(2))
-        passes(alone(2), (0,))
+        vec_scale(2, 0, 0, CW)
         vec_mask(pair(3))
+        vec_mask(pair(0))
+        quant(pair(3))
         place(grps, "gs", pair(2))
         for j, g in pair(2):
             scalar_scale(j, g, 0, CW)
+        for mt in range(MT):
+            quant_x(mt)
+        quant(pair(0))
+        for g in (0, 1, 3, 2):
+            passes(alone(g), (0,))
         evac(0)
-        vec_mask(pair(0))
-        quant(pair(3))
         passes(pair(3), (1,))
+        passes(pair(0), (1,))
         place(grpv, "gv", pair(1))
         vec_scale(1, 1, 0, CW)
-        quant(pair(0))
-        passes(pair(0), (1,))
         vec_scale(2, 1, 0, CW)
 
         def by_scalar(j):
@@ -249,9 +260,8 @@ def tile_ternarylinear_kernel(tc, x, kernel, out):
             place(grps, "gs", by_scalar(j))
             place(grpv, "gv", by_vector(j))
             scalar_scale(j, 3, 0, WIDTHS[j])
-            scalar_scale(j, 2, 0, WIDTHS[j])
-            if share(j):
-                scalar_scale(j, 1, 0, share(j))
+            if j not in HELPED:
+                scalar_scale(j, 2, 0, WIDTHS[j])
 
         ahead_scalar(3)
         vec_mask(pair(2))
@@ -271,17 +281,27 @@ def tile_ternarylinear_kernel(tc, x, kernel, out):
                 quant(by_vector(j - 1))
                 passes(by_vector(j - 1), (j - 1,))
             ahead_scalar(j + 1)
-            evac(j - 2)
+            if j <= 5:
+                evac(j - 2)
+            if j >= 5:
+                evac(j - 1)
+            if share(j + 1 if j + 1 < NCH else 0) and j + 1 < NCH:
+                scalar_scale(j + 1, 1, 0, share(j + 1))
             if j == 4:
                 for g in (3, 2, 0, 1):
                     load_w(g, (7, 8), rawu, "rawu")
+            if j in HELPED:
+                vec_scale(j, 2, 0, WIDTHS[j])
             vec_mask(by_scalar(j))
-            vec_scale(j, 1, share(j), WIDTHS[j])
+            vec_scale(j, 1, share(j) if j > 3 else 0, WIDTHS[j])
             quant(by_scalar(j))
             passes(by_scalar(j), (j,))
-            vec_mask(by_vector(j))
-        quant(by_vector(NCH - 1))
-        passes(by_vector(NCH - 1), (NCH - 1,))
-        evac(NCH - 2)
-        evac_half(NCH - 1, 0, "scalar")
-        evac_half(NCH - 1, 1, "vector")
+            if j < NCH - 1:
+                vec_mask(by_vector(j))
+        for unit in by_vector(NCH - 1):
+            vec_mask((unit,))
+        for unit in by_vector(NCH - 1):
+            quant((unit,))
+            passes((unit,), (NCH - 1,))
+        for mt in (0, 2, 1, 3):
+            evac_one(NCH - 1, mt, "scalar" if mt < 2 else "vector")

@@ -217,19 +217,19 @@ def tile_ternarylinear_kernel(tc, x, kernel, out):
         vec_mask(alone(3))
         quant(alone(1))
         place(grps, "gs", pair(3))
-        for j, g in pair(3):
-            scalar_scale(j, g, 0, CW)
+        scalar_scale(2, 3, 0, CW)
+        place(grpv, "gv", pair(0))
+        scalar_scale(1, 0, 0, CW)
         for mt in range(MT):
             transpose_x(mt)
+        vec_scale(1, 3, 0, CW)
         vec_mask(alone(2))
         quant(alone(3))
-        place(grpv, "gv", pair(0))
-        vec_scale(1, 0, 0, CW)
         quant(alone(2))
-        vec_scale(2, 0, 0, CW)
         vec_mask(pair(3))
-        vec_mask(pair(0))
+        vec_scale(2, 0, 0, CW)
         quant(pair(3))
+        vec_mask(pair(0))
         place(grps, "gs", pair(2))
         for j, g in pair(2):
             scalar_scale(j, g, 0, CW)

from contextlib import ExitStack

import concourse.mybir as mybir
from concourse.masks import make_identity

FLOPS = 2 * 512 * 2048 * 4096

BF16 = mybir.dt.bfloat16
F32 = mybir.dt.float32
I32 = mybir.dt.int32
U32 = mybir.dt.uint32
U8 = mybir.dt.uint8
FP8X4 = mybir.dt.float8_e4m3fn_x4
ALU = mybir.AluOpType
ACT = mybir.ActivationFunctionType

P = 128
CW = 512
G = 4
MT = 4
UP = 6.65625
MASK = -0x3FFF4000
WIDTHS = (512, 512, 512, 512, 512, 512, 512, 256, 256)
NCH = 9
COL0 = (0, 512, 1024, 1536, 2048, 2560, 3072, 3584, 3840)
HELPED = (3,)
CSH = 64


def tile_ternarylinear_kernel(tc, x, kernel, out):
    nc = tc.nc
    with ExitStack() as ctx:
        const = ctx.enter_context(tc.tile_pool(name="const", bufs=1))
        rawu = ctx.enter_context(tc.tile_pool(name="rawu", bufs=8))
        raws = ctx.enter_context(tc.tile_pool(name="raws", bufs=8))
        grpv = ctx.enter_context(tc.tile_pool(name="grpv", bufs=3))
        grpm = ctx.enter_context(tc.tile_pool(name="grpm", bufs=2))
        grps = ctx.enter_context(tc.tile_pool(name="grps", bufs=3))
        codp = ctx.enter_context(tc.tile_pool(name="codp", bufs=6))
        stgp = ctx.enter_context(tc.tile_pool(name="stgp", bufs=8))
        psum = ctx.enter_context(tc.psum_pool(name="psum", bufs=1))
        ctx.enter_context(tc.manual_schedule())

        ident = const.tile([P, P], F32, name="ident")
        make_identity(nc, ident[:])
        xq = const.tile([P, MT, 512], U32, name="xq", align_bytes=64)
        xs = const.tile([P, MT, 512], U8, name="xs", align_bytes=64)

        raw = {}

        def load_w(g, chunks, pool, tag):
            c0 = COL0[chunks[0]]
            ncols = sum(WIDTHS[j] for j in chunks)
            t = pool.tile([P, 4, ncols], BF16, name=tag, tag=tag)
            nc.sync.dma_start(
                out=t[:],
                in_=kernel[512 * g : 512 * (g + 1), c0 : c0 + ncols].rearrange("(p t) c -> p t c", t=4),
            )
            for j in chunks:
                raw[(j, g)] = (t, COL0[j] - c0)

        for g in (0, 3, 1, 2):
            load_w(g, (0,), rawu, "rawu")
        for g in (3, 0):
            load_w(g, (1, 2), raws, "raws")
        xr = []
        for mt in range(MT):
            t = rawu.tile([P, 2048], BF16, name="rawu", tag="rawu")
            nc.sync.dma_start(out=t[:], in_=x[mt])
            xr.append(t)
        for g in (2, 1):
            load_w(g, (1, 2), raws, "raws")
        for g in (3, 0, 2, 1):
            load_w(g, (3, 4), raws, "raws")

        xg = []

        def transpose_x(mt):
            xw = xr[mt][:].bitcast(F32).rearrange("p (g w u) -> p g u w", g=G, u=2)
            xgt = stgp.tile([P, 2048], BF16, name="st", tag="st", align_bytes=64)
            xg.append(xgt)
            for h in range(2):
                bank = psum.tile([P, 4, P], F32, name="xb%d" % (2 * mt + h), tag="bank%d" % (2 * mt + h))
                for a in range(2):
                    for u in range(2):
                        nc.tensor.transpose(bank[:, 2 * a + u, :], xw[:, 2 * h + a, u, :], ident[:])
                dst = xgt[:].bitcast(F32)[:, 512 * h : 512 * (h + 1)].rearrange("p (a m u) -> p a m u", a=2, u=2)
                nc.scalar.copy(out=dst, in_=bank[:].rearrange("p (a u) m -> p a m u", a=2, u=2))

        def quant_x(mt):
            nc.vector.quantize_mx(out=xq[:, mt, :].bitcast(FP8X4), scales=xs[:, mt, :], in_=xg[mt][:])

        home = {}
        acc = {}
        done = {}

        def place(pool, tag, units):
            t = pool.tile([P, 2 * CW, 4], BF16, name=tag, tag=tag, align_bytes=64)
            c = 0
            for j, g in units:
                home[(j, g)] = (t, c)
                c += WIDTHS[j]

        def views(j, g, c0, c1):
            t, h = home[(j, g)]
            rt, o = raw[(j, g)]
            return (
                t[:, h + c0 : h + c1, :].rearrange("p (c i) t -> p c t i", i=4),
                rt[:, :, o + c0 : o + c1].rearrange("p t (c i) -> p c t i", i=4),
            )

        def scalar_scale(j, g, c0, c1):
            o, i = views(j, g, c0, c1)
            nc.scalar.activation(out=o, in_=i, func=ACT.Copy, scale=UP)

        def vec_scale(j, g, c0, c1):
            o, i = views(j, g, c0, c1)
            nc.vector.tensor_scalar(out=o, in0=i, scalar1=UP, scalar2=None, op0=ALU.mult)

        tern = {}
        codes = {}

        def columns(units):
            return sum(WIDTHS[j] for j, g in units)

        def vec_mask(units):
            w = columns(units)
            t0, c0 = home[units[0]]
            t = grpm.tile([P, 4 * CW], I32, name="gm", tag="gm", align_bytes=64)
            nc.vector.tensor_scalar(
                out=t[:, 0 : 2 * w],
                in0=t0[:].rearrange("p c t -> p (c t)").bitcast(I32)[:, 2 * c0 : 2 * (c0 + w)],
                scalar1=MASK,
                scalar2=None,
                op0=ALU.bitwise_and,
            )
            tern[units] = t

        def quant(units):
            w = columns(units)
            cod = codp.tile([P, 2 * CW], U32, name="cod", tag="cod", align_bytes=64)
            scl = codp.tile([P, 2 * CW], U8, name="scl", tag="scl", align_bytes=64)
            nc.vector.quantize_mx(
                out=cod[:, 0:w].bitcast(FP8X4), scales=scl[:, 0:w], in_=tern[units][:, 0 : 2 * w].bitcast(BF16)
            )
            codes[units] = (cod, scl)

        def passes(units, chunks):
            cod, scl = codes[units]
            for j, g in units:
                if j not in chunks:
                    continue
                w = WIDTHS[j]
                c = home[(j, g)][1] - home[units[0]][1]
                done[j] = done.get(j, 0) + 1
                if done[j] == 1:
                    acc[j] = []
                    for mt in range(MT):
                        k = (MT * j + mt) % 8
                        bank = psum.tile([P, CW], F32, name="acc%d" % k, tag="bank%d" % k)
                        acc[j].append(bank)
                for mt in range(MT):
                    nc.tensor.matmul_mx(
                        out=acc[j][mt][:, 0:w],
                        lhsT=xq[:, mt, P * g : P * (g + 1)].bitcast(FP8X4),
                        lhsT_scale=xs[:, mt, P * g : P * (g + 1)],
                        rhs=cod[:, c : c + w].bitcast(FP8X4),
                        rhs_scale=scl[:, c : c + w],
                        start=(done[j] == 1),
                        stop=(done[j] == G),
                    )

        def evac_half(j, half, engine):
            w = WIDTHS[j]
            st = stgp.tile([P, 2, CW], F32, name="st", tag="st", align_bytes=64)
            for u in range(2):
                if engine == "vector":
                    nc.vector.tensor_scalar(
                        out=st[:, u, 0:w], in0=acc[j][2 * half + u][:, 0:w], scalar1=0.5, scalar2=None, op0=ALU.mult
                    )
                else:
                    nc.scalar.activation(out=st[:, u, 0:w], in_=acc[j][2 * half + u][:, 0:w], func=ACT.Copy, scale=0.5)
            nc.sync.dma_start(
                out=out[2 * half : 2 * half + 2, :, COL0[j] : COL0[j] + w].rearrange("b s n -> s b n"), in_=st[:, :, 0:w]
            )

        def evac_one(j, mt, engine):
            w = WIDTHS[j]
            st = stgp.tile([P, 2, CW], F32, name="st", tag="st", align_bytes=64)
            if engine == "vector":
                nc.vector.tensor_scalar(
                    out=st[:, 0, 0:w], in0=acc[j][mt][:, 0:w], scalar1=0.5, scalar2=None, op0=ALU.mult
                )
            else:
                nc.scalar.activation(out=st[:, 0, 0:w], in_=acc[j][mt][:, 0:w], func=ACT.Copy, scale=0.5)
            nc.sync.dma_start(out=out[mt, :, COL0[j] : COL0[j] + w], in_=st[:, 0, 0:w])

        def evac(j):
            evac_half(j, 0, "scalar")
            evac_half(j, 1, "scalar")

        def alone(g):
            return ((0, g),)

        for g in range(G):
            place(grpv if g < 2 else grps, "gv" if g < 2 else "gs", alone(g))
        def pair(g):
            return ((1, g), (2, g))

        vec_scale(0, 0, 0, CW)
        scalar_scale(0, 3, 0, CW)
        vec_scale(0, 1, 0, CW)
        vec_mask(alone(0))
        scalar_scale(0, 2, 0, CW)
        vec_mask(alone(1))
        quant(alone(0))
        vec_mask(alone(3))
        quant(alone(1))
        place(grps, "gs", pair(3))
        scalar_scale(2, 3, 0, CW)
        place(grpv, "gv", pair(0))
        scalar_scale(1, 0, 0, CW)
        for mt in range(MT):
            transpose_x(mt)
        vec_scale(1, 3, 0, CW)
        vec_mask(alone(2))
        quant(alone(3))
        quant(alone(2))
        vec_mask(pair(3))
        vec_scale(2, 0, 0, CW)
        quant(pair(3))
        vec_mask(pair(0))
        place(grps, "gs", pair(2))
        for j, g in pair(2):
            scalar_scale(j, g, 0, CW)
        for mt in range(MT):
            quant_x(mt)
        quant(pair(0))
        for g in (0, 1, 3, 2):
            passes(alone(g), (0,))
        evac(0)
        passes(pair(3), (1,))
        passes(pair(0), (1,))
        place(grpv, "gv", pair(1))
        vec_scale(1, 1, 0, CW)
        vec_scale(2, 1, 0, CW)

        def by_scalar(j):
            return ((j, 3), (j, 2))

        def by_vector(j):
            return ((j, 0), (j, 1))

        def share(j):
            return CSH * WIDTHS[j] // CW

        def ahead_scalar(j):
            if j >= NCH:
                return
            place(grps, "gs", by_scalar(j))
            place(grpv, "gv", by_vector(j))
            scalar_scale(j, 3, 0, WIDTHS[j])
            if j not in HELPED:
                scalar_scale(j, 2, 0, WIDTHS[j])

        ahead_scalar(3)
        vec_mask(pair(2))
        vec_mask(pair(1))
        quant(pair(2))
        passes(pair(2), (1,))
        for j in range(3, NCH):
            vec_scale(j, 0, 0, WIDTHS[j])
            if j == 3:
                quant(pair(1))
                passes(pair(1), (1,))
                for g in (3, 0, 2, 1):
                    passes(pair(g), (2,))
                for g in (3, 2, 0, 1):
                    load_w(g, (5, 6), raws, "raws")
            else:
                quant(by_vector(j - 1))
                passes(by_vector(j - 1), (j - 1,))
            ahead_scalar(j + 1)
            if j <= 5:
                evac(j - 2)
            if j >= 5:
                evac(j - 1)
            if share(j + 1 if j + 1 < NCH else 0) and j + 1 < NCH:
                scalar_scale(j + 1, 1, 0, share(j + 1))
            if j == 4:
                for g in (3, 2, 0, 1):
                    load_w(g, (7, 8), rawu, "rawu")
            if j in HELPED:
                vec_scale(j, 2, 0, WIDTHS[j])
            vec_mask(by_scalar(j))
            vec_scale(j, 1, share(j) if j > 3 else 0, WIDTHS[j])
            quant(by_scalar(j))
            passes(by_scalar(j), (j,))
            if j < NCH - 1:
                vec_mask(by_vector(j))
        for unit in by_vector(NCH - 1):
            vec_mask((unit,))
        for unit in by_vector(NCH - 1):
            quant((unit,))
            passes((unit,), (NCH - 1,))
        for mt in (0, 2, 1, 3):
            evac_one(NCH - 1, mt, "scalar" if mt < 2 else "vector")
